import numpy as np
import ml_dtypes


def mxq(x, axis, fmt="e4m3"):
    dtype, down = {"e4m3": (ml_dtypes.float8_e4m3fn, 7), "e5m2": (ml_dtypes.float8_e5m2, 14)}[fmt]
    v = np.moveaxis(np.asarray(x, np.float32).astype(ml_dtypes.bfloat16).astype(np.float64), axis, -1)
    blocks = v.reshape(v.shape[:-1] + (-1, 32))
    amax = np.abs(blocks).max(-1, keepdims=True)
    byte = np.maximum(np.where(amax > 0, np.frexp(amax)[1] - 1 + 127, 0) - down, 1)
    scale = np.exp2(byte - 127.0)
    codes = (blocks / scale).astype(np.float32).astype(dtype).astype(np.float64)
    return np.moveaxis((codes * scale).reshape(v.shape), -1, axis)


WIDE = False


def mx_kscale(k):
    if not WIDE:
        return np.ones(k)
    levels = np.array([10, -10, 5, -5, 0])
    a = np.random.permutation(np.resize(levels, k // 512 * 4)).reshape(k // 512, 4)
    idx = np.arange(k)
    return np.exp2(a[idx // 512, idx % 128 // 32])


BF16 = ml_dtypes.bfloat16


def bf(x):
    return np.asarray(x, np.float32).astype(BF16)


def f64(x):
    return np.asarray(x).astype(np.float64)


E2M1 = np.array([0.0, 0.5, 1.0, 1.5, 2.0, 3.0, 4.0, 6.0, -0.0, -0.5, -1.0, -1.5, -2.0, -3.0, -4.0, -6.0])


def pack_weight(w, fmt):
    k, n = w.shape
    w = f64(bf(w)).reshape(k // 32, 32, n)
    amax = np.abs(w).max(1)
    if fmt == "e4m3":
        byte = np.frexp(amax)[1] - 1 + 127 - 7
    else:
        mant, ex = np.frexp(amax / 6.0)
        byte = np.where(mant > 0.5, ex, ex - 1) + 127
    byte = np.clip(np.where(amax > 0, byte, 1), 1, 254)
    scaled = (w * np.exp2(127.0 - byte)[:, None, :]).reshape(k, n).astype(np.float32)
    by_word = np.ascontiguousarray(scaled.reshape(k // 512, 128, 4, n).transpose(0, 1, 3, 2))
    if fmt == "e4m3":
        words = by_word.astype(ml_dtypes.float8_e4m3fn).view(np.uint8)
    else:
        c = by_word.astype(ml_dtypes.float4_e2m1fn).view(np.uint8) & 0xF
        words = c[..., 0::2] | (c[..., 1::2] << 4)
    return np.ascontiguousarray(words), np.ascontiguousarray(byte.astype(np.uint8).reshape(k // 512, 16, n))


def unpack_weight(words, scales, fmt):
    g, p, n, _ = words.shape
    if fmt == "e4m3":
        vals = np.ascontiguousarray(words).view(ml_dtypes.float8_e4m3fn).astype(np.float64)
    else:
        nib = np.empty((g, p, n, 4), np.uint8)
        nib[..., 0::2] = words & 0xF
        nib[..., 1::2] = words >> 4
        vals = E2M1[nib]
    vals = vals * np.repeat(np.exp2(scales.astype(np.float64) - 127.0), 8, axis=1)[..., None]
    return vals.transpose(0, 1, 3, 2).reshape(g * 512, n)

def pack4(w):
    words, scales = pack_weight(w, "e2m1")
    return words.reshape(words.shape[0], 128, -1), scales


def unpack4(words, scales):
    return unpack_weight(words.reshape(words.shape[0], 128, -1, 2), scales, "e2m1")


BATCH, V_NODES, DEG = 512, 512, 4
EDGES = V_NODES * DEG


def _build_masks():
    v_of_edge = np.repeat(np.arange(V_NODES), DEG)
    input_mask = (np.arange(V_NODES)[:, None] == v_of_edge[None, :]).astype(np.float64)
    same_v = v_of_edge[:, None] == v_of_edge[None, :]
    prev_mask = (same_v & ~np.eye(EDGES, dtype=bool)).astype(np.float64)
    return input_mask, prev_mask


def setup_inputs():
    s, t = mx_kscale(V_NODES), mx_kscale(EDGES)
    input_mask, prev_mask = _build_masks()
    input_mask = input_mask + 0.02 * np.random.standard_normal((V_NODES, EDGES))
    prev_mask = prev_mask + 0.02 * np.random.standard_normal((EDGES, EDGES))
    x_in = bf(np.random.standard_normal((BATCH, V_NODES)) * s)
    x_prev = bf(np.random.standard_normal((BATCH, EDGES)) * t)
    input_mask_words, input_mask_scales = pack4(input_mask / s[:, None])
    prev_mask_words, prev_mask_scales = pack4(prev_mask / t[:, None])
    return {"x_in": x_in,
            "x_prev": x_prev,
            "input_mask_words": input_mask_words,
            "input_mask_scales": input_mask_scales,
            "prev_mask_words": prev_mask_words,
            "prev_mask_scales": prev_mask_scales}


def reference(x_in, x_prev, input_mask_words, input_mask_scales, prev_mask_words, prev_mask_scales):
    from_input = mxq(f64(x_in), 1, "e4m3") @ unpack4(input_mask_words, input_mask_scales)
    from_prev = mxq(f64(x_prev), 1, "e4m3") @ unpack4(prev_mask_words, prev_mask_scales)
    return from_input + from_prev

@@ -1,0 +1,166 @@
+from contextlib import ExitStack
+
+import concourse.mybir as mybir
+from concourse.masks import make_identity
+
+F32 = mybir.dt.float32
+BF16 = mybir.dt.bfloat16
+I32 = mybir.dt.int32
+U32 = mybir.dt.uint32
+U8 = mybir.dt.uint8
+FP8X4 = mybir.dt.float8_e4m3fn_x4
+FP4X4 = mybir.dt.float4_e2m1fn_x4
+
+P = 128
+BATCH = 512
+K_IN = 512
+K_PREV = 2048
+N_OUT = 2048
+N_TILE = 512
+M_TILES = BATCH // P
+PASSES = (K_IN + K_PREV) // 512
+FLOPS = 2 * BATCH * (K_IN + K_PREV) * N_OUT
+
+BANK_ORDER = (2, 3, 4, 5, 6, 7, 0, 1)
+TILE_ORDER = ((0, 0), (0, 1), (1, 0), (1, 1), (0, 2), (0, 3), (1, 2), (1, 3))
+
+
+def tile_oddlayer_kernel(
+    tc,
+    x_in,
+    x_prev,
+    input_mask_words,
+    input_mask_scales,
+    prev_mask_words,
+    prev_mask_scales,
+    out,
+):
+    nc = tc.nc
+    with ExitStack() as ctx:
+        keep = ctx.enter_context(tc.tile_pool(name="keep", bufs=1))
+        psum = ctx.enter_context(tc.psum_pool(name="psum", bufs=1))
+        ctx.enter_context(tc.manual_schedule())
+
+        ident = keep.tile([P, P], F32, name="ident")
+        make_identity(nc, ident[:])
+
+        plane0 = keep.tile([P, 1, N_OUT], U8, name="plane0", align_bytes=64)
+        plane12 = keep.tile([P, 2, N_OUT], U8, name="plane12", align_bytes=64)
+        plane34 = keep.tile([P, 2, N_OUT], U8, name="plane34", align_bytes=64)
+        for plane in (plane0, plane12, plane34):
+            nc.vector.memset(plane[:].rearrange("p g n -> p (g n)").bitcast(I32), 0)
+
+        def w_scale(g, n):
+            plane, j = ((plane0, 0), (plane12, 0), (plane12, 1), (plane34, 0), (plane34, 1))[g]
+            return plane[:, j, n * N_TILE : (n + 1) * N_TILE]
+
+        xin_raw = keep.tile([P, M_TILES, K_IN], BF16, name="xin_raw")
+        nc.sync.dma_start(out=xin_raw[:], in_=x_in.rearrange("(a p) k -> p a k", p=P))
+        xp_raw = []
+        for mi in range(M_TILES):
+            t = keep.tile([P, K_PREV], BF16, name="xp_raw%d" % mi)
+            nc.sync.dma_start(out=t[:], in_=x_prev[mi * P : (mi + 1) * P, :])
+            xp_raw.append(t)
+
+        def load_scales(plane, src):
+            for r in range(4):
+                nc.sync.dma_start(
+                    out=plane[r:P:32, :, :].bitcast(I32),
+                    in_=src[:, r:16:4, :].rearrange("g q n -> q g n").bitcast(I32),
+                )
+
+        w = [keep.tile([P, 2 * N_OUT], U8, name="w%d" % g, align_bytes=64) for g in range(PASSES)]
+
+        def load_words(g, lo, hi):
+            src = input_mask_words[0, :, :] if g == 0 else prev_mask_words[g - 1, :, :]
+            nc.sync.dma_start(out=w[g][:, lo:hi].bitcast(I32), in_=src[:, lo:hi].bitcast(I32))
+
+        load_scales(plane0, input_mask_scales)
+        load_words(0, 0, N_OUT)
+        load_words(0, N_OUT, 2 * N_OUT)
+        load_scales(plane12, prev_mask_scales[0:2, :, :])
+        load_words(1, 0, 2 * N_OUT)
+        load_words(2, 0, 2 * N_OUT)
+        load_scales(plane34, prev_mask_scales[2:4, :, :])
+        load_words(3, 0, 2 * N_OUT)
+        load_words(4, 0, 2 * N_OUT)
+
+        grouped = [keep.tile([P, 2048], BF16, name="grouped%d" % i, align_bytes=64) for i in range(5)]
+        codes = [keep.tile([P, 512], U32, name="codes%d" % i, align_bytes=64) for i in range(5)]
+        xsc = [keep.tile([P, 512], U8, name="xsc%d" % i, align_bytes=64) for i in range(5)]
+
+        def quantise(i):
+            nc.vector.quantize_mx(out=codes[i][:].bitcast(FP8X4), scales=xsc[i][:], in_=grouped[i][:])
+
+        for i in range(5):
+            for half in range(2):
+                bank = (2 * i + half) % 8
+                pt = psum.tile([P, 2, 2, P], F32, name="pt%d_%d" % (i, half), tag="bank%d" % bank)
+                for a in range(2):
+                    blk = 2 * half + a
+                    if i == 0:
+                        words = xin_raw[:, blk, :].bitcast(F32)
+                    else:
+                        words = xp_raw[i - 1][:, 512 * blk : 512 * (blk + 1)].bitcast(F32)
+                    for u in range(2):
+                        nc.tensor.transpose(pt[:, a, u, :], words[:, u:256:2], ident[:])
+                dst = (
+                    grouped[i][:]
+                    .bitcast(F32)[:, 512 * half : 512 * (half + 1)]
+                    .rearrange("p (a m u) -> p a m u", a=2, u=2)
+                )
+                src = pt[:].rearrange("p a u m -> p a m u")
+                if half == 0:
+                    nc.scalar.copy(out=dst, in_=src)
+                else:
+                    nc.vector.tensor_copy(out=dst, in_=src)
+            if i > 0:
+                quantise(i - 1)
+        quantise(4)
+
+        def x_operand(g, mi):
+            if g == 0:
+                i, blk = 0, mi
+            else:
+                i, blk = 1 + mi, g - 1
+            cols = slice(blk * P, (blk + 1) * P)
+            return codes[i][:, cols].bitcast(FP8X4), xsc[i][:, cols]
+
+        def mx_pass(acc, g, mi, n):
+            lhsT, lhsT_scale = x_operand(g, mi)
+            nc.tensor.matmul_mx(
+                out=acc[:],
+                lhsT=lhsT,
+                lhsT_scale=lhsT_scale,
+                rhs=w[g][:, n * 2 * N_TILE : (n + 1) * 2 * N_TILE].bitcast(FP4X4),
+                rhs_scale=w_scale(g, n),
+                start=(g == 0),
+                stop=(g == PASSES - 1),
+            )
+
+        def finish(acc, mi, n, j):
+            res = keep.tile([P, N_TILE], F32, name="res%d_%d" % (mi, n))
+            if j % 2 == 0:
+                nc.scalar.copy(out=res[:], in_=acc[:])
+            else:
+                nc.vector.tensor_copy(out=res[:], in_=acc[:])
+            nc.sync.dma_start(
+                out=out[mi * P : (mi + 1) * P, n * N_TILE : (n + 1) * N_TILE], in_=res[:]
+            )
+
+        accs = [
+            psum.tile([P, N_TILE], F32, name="accA%d" % j, tag="bank%d" % BANK_ORDER[j])
+            for j in range(8)
+        ]
+        for g in range(PASSES):
+            for j, (mi, n) in enumerate(TILE_ORDER):
+                mx_pass(accs[j], g, mi, n)
+        for j, (mi, n) in enumerate(TILE_ORDER):
+            finish(accs[j], mi, n, j)
+
+        for j, (mr, n) in enumerate(TILE_ORDER):
+            mi = 2 + mr
+            acc = psum.tile([P, N_TILE], F32, name="accB%d" % j, tag="bank%d" % BANK_ORDER[j])
+            for g in range(PASSES):
+                mx_pass(acc, g, mi, n)
+            finish(acc, mi, n, j)

@@ -50,16 +50,21 @@ def tile_oddlayer_kernel(
         for plane in (plane0, plane12, plane34):
             nc.vector.memset(plane[:].rearrange("p g n -> p (g n)").bitcast(I32), 0)
 
+        def w_plane(g):
+            return ((plane0, 0), (plane12, 0), (plane12, 1), (plane34, 0), (plane34, 1))[g]
+
         def w_scale(g, n):
-            plane, j = ((plane0, 0), (plane12, 0), (plane12, 1), (plane34, 0), (plane34, 1))[g]
+            plane, j = w_plane(g)
             return plane[:, j, n * N_TILE : (n + 1) * N_TILE]
 
         xin_raw = keep.tile([P, M_TILES, K_IN], BF16, name="xin_raw")
-        nc.sync.dma_start(out=xin_raw[:], in_=x_in.rearrange("(a p) k -> p a k", p=P))
+        nc.sync.dma_start(out=xin_raw[:], in_=x_in.rearrange("(p a) k -> p a k", a=M_TILES))
+        xp_rows = x_prev.rearrange("(p a) k -> a p k", a=M_TILES)
+        out_rows = out.rearrange("(p a) n -> a p n", a=M_TILES)
         xp_raw = []
         for mi in range(M_TILES):
             t = keep.tile([P, K_PREV], BF16, name="xp_raw%d" % mi)
-            nc.sync.dma_start(out=t[:], in_=x_prev[mi * P : (mi + 1) * P, :])
+            nc.sync.dma_start(out=t[:], in_=xp_rows[mi, :, :])
             xp_raw.append(t)
 
         def load_scales(plane, src):
@@ -144,9 +149,7 @@ def tile_oddlayer_kernel(
                 nc.scalar.copy(out=res[:], in_=acc[:])
             else:
                 nc.vector.tensor_copy(out=res[:], in_=acc[:])
-            nc.sync.dma_start(
-                out=out[mi * P : (mi + 1) * P, n * N_TILE : (n + 1) * N_TILE], in_=res[:]
-            )
+            nc.sync.dma_start(out=out_rows[mi, :, n * N_TILE : (n + 1) * N_TILE], in_=res[:])
 
         accs = [
             psum.tile([P, N_TILE], F32, name="accA%d" % j, tag="bank%d" % BANK_ORDER[j])
@@ -158,9 +161,33 @@ def tile_oddlayer_kernel(
         for j, (mi, n) in enumerate(TILE_ORDER):
             finish(accs[j], mi, n, j)
 
-        for j, (mr, n) in enumerate(TILE_ORDER):
+        for j, (mr, n) in enumerate(TILE_ORDER[:7]):
             mi = 2 + mr
             acc = psum.tile([P, N_TILE], F32, name="accB%d" % j, tag="bank%d" % BANK_ORDER[j])
             for g in range(PASSES):
                 mx_pass(acc, g, mi, n)
             finish(acc, mi, n, j)
+
+        mi, n = 2 + TILE_ORDER[7][0], TILE_ORDER[7][1]
+        last = keep.tile([P, N_TILE], F32, name="last")
+        for q in range(4):
+            acc = psum.tile([P, P], F32, name="accL%d" % q, tag="bank%d" % BANK_ORDER[(7 + q) % 8])
+            c0 = n * N_TILE + q * P
+            for g in range(PASSES):
+                lhsT, lhsT_scale = x_operand(g, mi)
+                plane, jj = w_plane(g)
+                nc.tensor.matmul_mx(
+                    out=acc[:],
+                    lhsT=lhsT,
+                    lhsT_scale=lhsT_scale,
+                    rhs=w[g][:, 2 * c0 : 2 * (c0 + P)].bitcast(FP4X4),
+                    rhs_scale=plane[:, jj, c0 : c0 + P],
+                    start=(g == 0),
+                    stop=(g == PASSES - 1),
+                )
+            part = last[:, q * P : (q + 1) * P]
+            if q % 2 == 0:
+                nc.vector.tensor_copy(out=part, in_=acc[:])
+            else:
+                nc.scalar.copy(out=part, in_=acc[:])
+            nc.sync.dma_start(out=out_rows[mi, :, c0 : c0 + P], in_=part)

@@ -21,8 +21,9 @@ M_TILES = BATCH // P
 PASSES = (K_IN + K_PREV) // 512
 FLOPS = 2 * BATCH * (K_IN + K_PREV) * N_OUT
 
-BANK_ORDER = (2, 3, 4, 5, 6, 7, 0, 1)
-TILE_ORDER = ((0, 0), (0, 1), (1, 0), (1, 1), (0, 2), (0, 3), (1, 2), (1, 3))
+BANKS = (6, 7, 0, 1, 2, 3, 4, 5)
+ROUND_A = ((0, 0), (0, 1), (1, 0), (1, 1), (0, 2), (0, 3), (1, 2), (1, 3))
+ROUND_B = ((2, 0, 4), (2, 1, 5), (2, 2, 6), (2, 3, 7), (3, 0, 0), (3, 1, 1), (3, 2, 2), (3, 3, 3))
 
 
 def tile_oddlayer_kernel(
@@ -50,22 +51,18 @@ def tile_oddlayer_kernel(
         for plane in (plane0, plane12, plane34):
             nc.vector.memset(plane[:].rearrange("p g n -> p (g n)").bitcast(I32), 0)
 
-        def w_plane(g):
-            return ((plane0, 0), (plane12, 0), (plane12, 1), (plane34, 0), (plane34, 1))[g]
-
         def w_scale(g, n):
-            plane, j = w_plane(g)
+            plane, j = ((plane0, 0), (plane12, 0), (plane12, 1), (plane34, 0), (plane34, 1))[g]
             return plane[:, j, n * N_TILE : (n + 1) * N_TILE]
 
-        xin_raw = keep.tile([P, M_TILES, K_IN], BF16, name="xin_raw")
-        nc.sync.dma_start(out=xin_raw[:], in_=x_in.rearrange("(p a) k -> p a k", a=M_TILES))
         xp_rows = x_prev.rearrange("(p a) k -> a p k", a=M_TILES)
         out_rows = out.rearrange("(p a) n -> a p n", a=M_TILES)
-        xp_raw = []
-        for mi in range(M_TILES):
-            t = keep.tile([P, K_PREV], BF16, name="xp_raw%d" % mi)
-            nc.sync.dma_start(out=t[:], in_=xp_rows[mi, :, :])
-            xp_raw.append(t)
+        xin_raw = keep.tile([P, M_TILES, K_IN], BF16, name="xin_raw")
+        xp_raw = [keep.tile([P, K_PREV], BF16, name="xp_raw%d" % mi) for mi in range(M_TILES)]
+        w = [keep.tile([P, 2 * N_OUT], U8, name="w%d" % g, align_bytes=64) for g in range(PASSES)]
+
+        def load_x_prev(mi):
+            nc.sync.dma_start(out=xp_raw[mi][:], in_=xp_rows[mi, :, :])
 
         def load_scales(plane, src):
             for r in range(4):
@@ -74,12 +71,13 @@ def tile_oddlayer_kernel(
                     in_=src[:, r:16:4, :].rearrange("g q n -> q g n").bitcast(I32),
                 )
 
-        w = [keep.tile([P, 2 * N_OUT], U8, name="w%d" % g, align_bytes=64) for g in range(PASSES)]
-
         def load_words(g, lo, hi):
             src = input_mask_words[0, :, :] if g == 0 else prev_mask_words[g - 1, :, :]
             nc.sync.dma_start(out=w[g][:, lo:hi].bitcast(I32), in_=src[:, lo:hi].bitcast(I32))
 
+        nc.sync.dma_start(out=xin_raw[:], in_=x_in.rearrange("(p a) k -> p a k", a=M_TILES))
+        load_x_prev(0)
+        load_x_prev(1)
         load_scales(plane0, input_mask_scales)
         load_words(0, 0, N_OUT)
         load_words(0, N_OUT, 2 * N_OUT)
@@ -89,6 +87,8 @@ def tile_oddlayer_kernel(
         load_scales(plane34, prev_mask_scales[2:4, :, :])
         load_words(3, 0, 2 * N_OUT)
         load_words(4, 0, 2 * N_OUT)
+        load_x_prev(2)
+        load_x_prev(3)
 
         grouped = [keep.tile([P, 2048], BF16, name="grouped%d" % i, align_bytes=64) for i in range(5)]
         codes = [keep.tile([P, 512], U32, name="codes%d" % i, align_bytes=64) for i in range(5)]
@@ -97,18 +97,12 @@ def tile_oddlayer_kernel(
         def quantise(i):
             nc.vector.quantize_mx(out=codes[i][:].bitcast(FP8X4), scales=xsc[i][:], in_=grouped[i][:])
 
-        for i in range(5):
+        def flip(i, banks, word_cols):
             for half in range(2):
-                bank = (2 * i + half) % 8
-                pt = psum.tile([P, 2, 2, P], F32, name="pt%d_%d" % (i, half), tag="bank%d" % bank)
+                pt = psum.tile([P, 2, 2, P], F32, name="pt%d_%d" % (i, half), tag="bank%d" % banks[half])
                 for a in range(2):
-                    blk = 2 * half + a
-                    if i == 0:
-                        words = xin_raw[:, blk, :].bitcast(F32)
-                    else:
-                        words = xp_raw[i - 1][:, 512 * blk : 512 * (blk + 1)].bitcast(F32)
                     for u in range(2):
-                        nc.tensor.transpose(pt[:, a, u, :], words[:, u:256:2], ident[:])
+                        nc.tensor.transpose(pt[:, a, u, :], word_cols(2 * half + a, u), ident[:])
                 dst = (
                     grouped[i][:]
                     .bitcast(F32)[:, 512 * half : 512 * (half + 1)]
@@ -119,9 +113,36 @@ def tile_oddlayer_kernel(
                     nc.scalar.copy(out=dst, in_=src)
                 else:
                     nc.vector.tensor_copy(out=dst, in_=src)
-            if i > 0:
-                quantise(i - 1)
-        quantise(4)
+
+        def strided_cols(i):
+            def cols(blk, u):
+                if i == 0:
+                    return xin_raw[:, blk, :].bitcast(F32)[:, u:256:2]
+                return xp_raw[i - 1][:, 512 * blk : 512 * (blk + 1)].bitcast(F32)[:, u:256:2]
+
+            return cols
+
+        def sorted_cols(sw):
+            def cols(blk, u):
+                return sw[:, blk, u, :]
+
+            return cols
+
+        flip(0, (0, 1), strided_cols(0))
+        flip(1, (2, 3), strided_cols(1))
+        quantise(0)
+        flip(2, (4, 5), strided_cols(2))
+        quantise(1)
+        quantise(2)
+
+        sorted_words = []
+        for mi in (2, 3):
+            sw = keep.tile([P, 4, 2, P], F32, name="sorted%d" % mi)
+            nc.vector.tensor_copy(
+                out=sw[:],
+                in_=xp_raw[mi][:].bitcast(F32).rearrange("p (b j u) -> p b u j", b=4, u=2),
+            )
+            sorted_words.append(sw)
 
         def x_operand(g, mi):
             if g == 0:
@@ -152,42 +173,26 @@ def tile_oddlayer_kernel(
             nc.sync.dma_start(out=out_rows[mi, :, n * N_TILE : (n + 1) * N_TILE], in_=res[:])
 
         accs = [
-            psum.tile([P, N_TILE], F32, name="accA%d" % j, tag="bank%d" % BANK_ORDER[j])
-            for j in range(8)
+            psum.tile([P, N_TILE], F32, name="accA%d" % j, tag="bank%d" % BANKS[j]) for j in range(8)
         ]
         for g in range(PASSES):
-            for j, (mi, n) in enumerate(TILE_ORDER):
+            for j, (mi, n) in enumerate(ROUND_A):
                 mx_pass(accs[j], g, mi, n)
-        for j, (mi, n) in enumerate(TILE_ORDER):
+        for j, (mi, n) in enumerate(ROUND_A):
             finish(accs[j], mi, n, j)
 
-        for j, (mr, n) in enumerate(TILE_ORDER[:7]):
-            mi = 2 + mr
-            acc = psum.tile([P, N_TILE], F32, name="accB%d" % j, tag="bank%d" % BANK_ORDER[j])
-            for g in range(PASSES):
-                mx_pass(acc, g, mi, n)
-            finish(acc, mi, n, j)
+        for s, mi in enumerate((2, 3)):
+            flip(1 + mi, (BANKS[2 * s], BANKS[2 * s + 1]), sorted_cols(sorted_words[s]))
+        quantise(3)
+        quantise(4)
 
-        mi, n = 2 + TILE_ORDER[7][0], TILE_ORDER[7][1]
-        last = keep.tile([P, N_TILE], F32, name="last")
-        for q in range(4):
-            acc = psum.tile([P, P], F32, name="accL%d" % q, tag="bank%d" % BANK_ORDER[(7 + q) % 8])
-            c0 = n * N_TILE + q * P
-            for g in range(PASSES):
-                lhsT, lhsT_scale = x_operand(g, mi)
-                plane, jj = w_plane(g)
-                nc.tensor.matmul_mx(
-                    out=acc[:],
-                    lhsT=lhsT,
-                    lhsT_scale=lhsT_scale,
-                    rhs=w[g][:, 2 * c0 : 2 * (c0 + P)].bitcast(FP4X4),
-                    rhs_scale=plane[:, jj, c0 : c0 + P],
-                    start=(g == 0),
-                    stop=(g == PASSES - 1),
-                )
-            part = last[:, q * P : (q + 1) * P]
-            if q % 2 == 0:
-                nc.vector.tensor_copy(out=part, in_=acc[:])
-            else:
-                nc.scalar.copy(out=part, in_=acc[:])
-            nc.sync.dma_start(out=out_rows[mi, :, c0 : c0 + P], in_=part)
+        accs = [
+            psum.tile([P, N_TILE], F32, name="accB%d" % j, tag="bank%d" % BANKS[b])
+            for j, (mi, n, b) in enumerate(ROUND_B)
+        ]
+        for j, (mi, n, b) in enumerate(ROUND_B):
+            mx_pass(accs[j], 0, mi, n)
+        for j, (mi, n, b) in enumerate(ROUND_B):
+            for g in range(1, PASSES):
+                mx_pass(accs[j], g, mi, n)
+            finish(accs[j], mi, n, j)

@@ -129,8 +129,8 @@ def tile_oddlayer_kernel(
             return cols
 
         flip(0, (0, 1), strided_cols(0))
-        flip(1, (2, 3), strided_cols(1))
         quantise(0)
+        flip(1, (2, 3), strided_cols(1))
         flip(2, (4, 5), strided_cols(2))
         quantise(1)
         quantise(2)

@@ -46,13 +46,14 @@ def tile_oddlayer_kernel(
         make_identity(nc, ident[:])
 
         plane0 = keep.tile([P, 1, N_OUT], U8, name="plane0", align_bytes=64)
-        plane12 = keep.tile([P, 2, N_OUT], U8, name="plane12", align_bytes=64)
+        plane1 = keep.tile([P, 1, N_OUT], U8, name="plane1", align_bytes=64)
+        plane2 = keep.tile([P, 1, N_OUT], U8, name="plane2", align_bytes=64)
         plane34 = keep.tile([P, 2, N_OUT], U8, name="plane34", align_bytes=64)
-        for plane in (plane0, plane12, plane34):
+        for plane in (plane0, plane1, plane2, plane34):
             nc.vector.memset(plane[:].rearrange("p g n -> p (g n)").bitcast(I32), 0)
 
         def w_scale(g, n):
-            plane, j = ((plane0, 0), (plane12, 0), (plane12, 1), (plane34, 0), (plane34, 1))[g]
+            plane, j = ((plane0, 0), (plane1, 0), (plane2, 0), (plane34, 0), (plane34, 1))[g]
             return plane[:, j, n * N_TILE : (n + 1) * N_TILE]
 
         xp_rows = x_prev.rearrange("(p a) k -> a p k", a=M_TILES)
@@ -81,8 +82,10 @@ def tile_oddlayer_kernel(
         load_scales(plane0, input_mask_scales)
         load_words(0, 0, N_OUT)
         load_words(0, N_OUT, 2 * N_OUT)
-        load_scales(plane12, prev_mask_scales[0:2, :, :])
-        load_words(1, 0, 2 * N_OUT)
+        load_scales(plane1, prev_mask_scales[0:1, :, :])
+        load_words(1, 0, N_OUT)
+        load_words(1, N_OUT, 2 * N_OUT)
+        load_scales(plane2, prev_mask_scales[1:2, :, :])
         load_words(2, 0, 2 * N_OUT)
         load_scales(plane34, prev_mask_scales[2:4, :, :])
         load_words(3, 0, 2 * N_OUT)

@@ -22,7 +22,7 @@ PASSES = (K_IN + K_PREV) // 512
 FLOPS = 2 * BATCH * (K_IN + K_PREV) * N_OUT
 
 BANKS = (6, 7, 0, 1, 2, 3, 4, 5)
-ROUND_A = ((0, 0), (0, 1), (1, 0), (1, 1), (0, 2), (0, 3), (1, 2), (1, 3))
+ROUND_A = ((0, 0), (1, 0), (0, 1), (1, 1), (0, 2), (1, 2), (0, 3), (1, 3))
 ROUND_B = ((2, 0, 4), (2, 1, 5), (2, 2, 6), (2, 3, 7), (3, 0, 0), (3, 1, 1), (3, 2, 2), (3, 3, 3))
 
 
@@ -48,12 +48,13 @@ def tile_oddlayer_kernel(
         plane0 = keep.tile([P, 1, N_OUT], U8, name="plane0", align_bytes=64)
         plane1 = keep.tile([P, 1, N_OUT], U8, name="plane1", align_bytes=64)
         plane2 = keep.tile([P, 1, N_OUT], U8, name="plane2", align_bytes=64)
-        plane34 = keep.tile([P, 2, N_OUT], U8, name="plane34", align_bytes=64)
-        for plane in (plane0, plane1, plane2, plane34):
+        plane3 = keep.tile([P, 1, N_OUT], U8, name="plane3", align_bytes=64)
+        plane4 = keep.tile([P, 1, N_OUT], U8, name="plane4", align_bytes=64)
+        for plane in (plane0, plane1, plane2, plane3, plane4):
             nc.vector.memset(plane[:].rearrange("p g n -> p (g n)").bitcast(I32), 0)
 
         def w_scale(g, n):
-            plane, j = ((plane0, 0), (plane1, 0), (plane2, 0), (plane34, 0), (plane34, 1))[g]
+            plane, j = ((plane0, 0), (plane1, 0), (plane2, 0), (plane3, 0), (plane4, 0))[g]
             return plane[:, j, n * N_TILE : (n + 1) * N_TILE]
 
         xp_rows = x_prev.rearrange("(p a) k -> a p k", a=M_TILES)
@@ -65,11 +66,11 @@ def tile_oddlayer_kernel(
         def load_x_prev(mi):
             nc.sync.dma_start(out=xp_raw[mi][:], in_=xp_rows[mi, :, :])
 
-        def load_scales(plane, src):
+        def load_scales(plane, src, lo=0, hi=N_OUT):
             for r in range(4):
                 nc.sync.dma_start(
-                    out=plane[r:P:32, :, :].bitcast(I32),
-                    in_=src[:, r:16:4, :].rearrange("g q n -> q g n").bitcast(I32),
+                    out=plane[r:P:32, :, lo:hi].bitcast(I32),
+                    in_=src[:, r:16:4, lo:hi].rearrange("g q n -> q g n").bitcast(I32),
                 )
 
         def load_words(g, lo, hi):
@@ -79,17 +80,23 @@ def tile_oddlayer_kernel(
         nc.sync.dma_start(out=xin_raw[:], in_=x_in.rearrange("(p a) k -> p a k", a=M_TILES))
         load_x_prev(0)
         load_x_prev(1)
-        load_scales(plane0, input_mask_scales)
-        load_words(0, 0, N_OUT)
+        load_scales(plane0, input_mask_scales, 0, N_OUT // 2)
+        load_words(0, 0, N_OUT // 2)
+        load_words(0, N_OUT // 2, N_OUT)
+        load_scales(plane0, input_mask_scales, N_OUT // 2, N_OUT)
         load_words(0, N_OUT, 2 * N_OUT)
         load_scales(plane1, prev_mask_scales[0:1, :, :])
         load_words(1, 0, N_OUT)
         load_words(1, N_OUT, 2 * N_OUT)
         load_scales(plane2, prev_mask_scales[1:2, :, :])
-        load_words(2, 0, 2 * N_OUT)
-        load_scales(plane34, prev_mask_scales[2:4, :, :])
-        load_words(3, 0, 2 * N_OUT)
-        load_words(4, 0, 2 * N_OUT)
+        load_words(2, 0, N_OUT)
+        load_words(2, N_OUT, 2 * N_OUT)
+        load_scales(plane3, prev_mask_scales[2:3, :, :])
+        load_words(3, 0, N_OUT)
+        load_words(3, N_OUT, 2 * N_OUT)
+        load_scales(plane4, prev_mask_scales[3:4, :, :])
+        load_words(4, 0, N_OUT)
+        load_words(4, N_OUT, 2 * N_OUT)
         load_x_prev(2)
         load_x_prev(3)
 

@@ -21,9 +21,8 @@ M_TILES = BATCH // P
 PASSES = (K_IN + K_PREV) // 512
 FLOPS = 2 * BATCH * (K_IN + K_PREV) * N_OUT
 
-BANKS = (6, 7, 0, 1, 2, 3, 4, 5)
-ROUND_A = ((0, 0), (1, 0), (0, 1), (1, 1), (0, 2), (1, 2), (0, 3), (1, 3))
-ROUND_B = ((2, 0, 4), (2, 1, 5), (2, 2, 6), (2, 3, 7), (3, 0, 0), (3, 1, 1), (3, 2, 2), (3, 3, 3))
+BANKS = (2, 3, 4, 5, 6, 7, 0, 1)
+SCALE_GROUPS = ((0, 1), (1, 2), (2, 3), (3, 5))
 
 
 def tile_oddlayer_kernel(
@@ -45,17 +44,11 @@ def tile_oddlayer_kernel(
         ident = keep.tile([P, P], F32, name="ident")
         make_identity(nc, ident[:])
 
-        plane0 = keep.tile([P, 1, N_OUT], U8, name="plane0", align_bytes=64)
-        plane1 = keep.tile([P, 1, N_OUT], U8, name="plane1", align_bytes=64)
-        plane2 = keep.tile([P, 1, N_OUT], U8, name="plane2", align_bytes=64)
-        plane3 = keep.tile([P, 1, N_OUT], U8, name="plane3", align_bytes=64)
-        plane4 = keep.tile([P, 1, N_OUT], U8, name="plane4", align_bytes=64)
-        for plane in (plane0, plane1, plane2, plane3, plane4):
-            nc.vector.memset(plane[:].rearrange("p g n -> p (g n)").bitcast(I32), 0)
-
-        def w_scale(g, n):
-            plane, j = ((plane0, 0), (plane1, 0), (plane2, 0), (plane3, 0), (plane4, 0))[g]
-            return plane[:, j, n * N_TILE : (n + 1) * N_TILE]
+        plane_of = []
+        for g0, g1 in SCALE_GROUPS:
+            planes = keep.tile([P, g1 - g0, N_OUT], U8, name="planes%d" % g0, align_bytes=64)
+            nc.vector.memset(planes[:].rearrange("p g n -> p (g n)").bitcast(I32), 0)
+            plane_of.extend([(planes, g - g0) for g in range(g0, g1)])
 
         xp_rows = x_prev.rearrange("(p a) k -> a p k", a=M_TILES)
         out_rows = out.rearrange("(p a) n -> a p n", a=M_TILES)
@@ -63,14 +56,13 @@ def tile_oddlayer_kernel(
         xp_raw = [keep.tile([P, K_PREV], BF16, name="xp_raw%d" % mi) for mi in range(M_TILES)]
         w = [keep.tile([P, 2 * N_OUT], U8, name="w%d" % g, align_bytes=64) for g in range(PASSES)]
 
-        def load_x_prev(mi):
-            nc.sync.dma_start(out=xp_raw[mi][:], in_=xp_rows[mi, :, :])
-
-        def load_scales(plane, src, lo=0, hi=N_OUT):
+        def load_scales(g0, g1):
+            src = input_mask_scales if g0 == 0 else prev_mask_scales[g0 - 1 : g1 - 1, :, :]
+            planes = plane_of[g0][0]
             for r in range(4):
                 nc.sync.dma_start(
-                    out=plane[r:P:32, :, lo:hi].bitcast(I32),
-                    in_=src[:, r:16:4, lo:hi].rearrange("g q n -> q g n").bitcast(I32),
+                    out=planes[r:P:32, :, :].bitcast(I32),
+                    in_=src[:, r:16:4, :].rearrange("g q n -> q g n").bitcast(I32),
                 )
 
         def load_words(g, lo, hi):
@@ -78,27 +70,19 @@ def tile_oddlayer_kernel(
             nc.sync.dma_start(out=w[g][:, lo:hi].bitcast(I32), in_=src[:, lo:hi].bitcast(I32))
 
         nc.sync.dma_start(out=xin_raw[:], in_=x_in.rearrange("(p a) k -> p a k", a=M_TILES))
-        load_x_prev(0)
-        load_x_prev(1)
-        load_scales(plane0, input_mask_scales, 0, N_OUT // 2)
-        load_words(0, 0, N_OUT // 2)
-        load_words(0, N_OUT // 2, N_OUT)
-        load_scales(plane0, input_mask_scales, N_OUT // 2, N_OUT)
+        for mi in range(M_TILES):
+            nc.sync.dma_start(out=xp_raw[mi][:], in_=xp_rows[mi, :, :])
+        load_scales(0, 1)
+        load_words(0, 0, N_OUT)
         load_words(0, N_OUT, 2 * N_OUT)
-        load_scales(plane1, prev_mask_scales[0:1, :, :])
+        load_scales(1, 2)
         load_words(1, 0, N_OUT)
         load_words(1, N_OUT, 2 * N_OUT)
-        load_scales(plane2, prev_mask_scales[1:2, :, :])
-        load_words(2, 0, N_OUT)
-        load_words(2, N_OUT, 2 * N_OUT)
-        load_scales(plane3, prev_mask_scales[2:3, :, :])
-        load_words(3, 0, N_OUT)
-        load_words(3, N_OUT, 2 * N_OUT)
-        load_scales(plane4, prev_mask_scales[3:4, :, :])
-        load_words(4, 0, N_OUT)
-        load_words(4, N_OUT, 2 * N_OUT)
-        load_x_prev(2)
-        load_x_prev(3)
+        load_scales(2, 3)
+        load_words(2, 0, 2 * N_OUT)
+        load_scales(3, 5)
+        load_words(3, 0, 2 * N_OUT)
+        load_words(4, 0, 2 * N_OUT)
 
         grouped = [keep.tile([P, 2048], BF16, name="grouped%d" % i, align_bytes=64) for i in range(5)]
         codes = [keep.tile([P, 512], U32, name="codes%d" % i, align_bytes=64) for i in range(5)]
@@ -107,12 +91,19 @@ def tile_oddlayer_kernel(
         def quantise(i):
             nc.vector.quantize_mx(out=codes[i][:].bitcast(FP8X4), scales=xsc[i][:], in_=grouped[i][:])
 
-        def flip(i, banks, word_cols):
+        for i in range(5):
             for half in range(2):
-                pt = psum.tile([P, 2, 2, P], F32, name="pt%d_%d" % (i, half), tag="bank%d" % banks[half])
+                pt = psum.tile(
+                    [P, 2, 2, P], F32, name="pt%d_%d" % (i, half), tag="bank%d" % ((2 * i + half) % 8)
+                )
                 for a in range(2):
+                    blk = 2 * half + a
+                    if i == 0:
+                        words = xin_raw[:, blk, :].bitcast(F32)
+                    else:
+                        words = xp_raw[i - 1][:, 512 * blk : 512 * (blk + 1)].bitcast(F32)
                     for u in range(2):
-                        nc.tensor.transpose(pt[:, a, u, :], word_cols(2 * half + a, u), ident[:])
+                        nc.tensor.transpose(pt[:, a, u, :], words[:, u:256:2], ident[:])
                 dst = (
                     grouped[i][:]
                     .bitcast(F32)[:, 512 * half : 512 * (half + 1)]
@@ -123,53 +114,22 @@ def tile_oddlayer_kernel(
                     nc.scalar.copy(out=dst, in_=src)
                 else:
                     nc.vector.tensor_copy(out=dst, in_=src)
+            if i > 0:
+                quantise(i - 1)
+        quantise(4)
 
-        def strided_cols(i):
-            def cols(blk, u):
-                if i == 0:
-                    return xin_raw[:, blk, :].bitcast(F32)[:, u:256:2]
-                return xp_raw[i - 1][:, 512 * blk : 512 * (blk + 1)].bitcast(F32)[:, u:256:2]
-
-            return cols
-
-        def sorted_cols(sw):
-            def cols(blk, u):
-                return sw[:, blk, u, :]
-
-            return cols
-
-        flip(0, (0, 1), strided_cols(0))
-        quantise(0)
-        flip(1, (2, 3), strided_cols(1))
-        flip(2, (4, 5), strided_cols(2))
-        quantise(1)
-        quantise(2)
-
-        sorted_words = []
-        for mi in (2, 3):
-            sw = keep.tile([P, 4, 2, P], F32, name="sorted%d" % mi)
-            nc.vector.tensor_copy(
-                out=sw[:],
-                in_=xp_raw[mi][:].bitcast(F32).rearrange("p (b j u) -> p b u j", b=4, u=2),
-            )
-            sorted_words.append(sw)
-
-        def x_operand(g, mi):
+        def mx_pass(acc, g, mi, n):
             if g == 0:
                 i, blk = 0, mi
             else:
                 i, blk = 1 + mi, g - 1
             cols = slice(blk * P, (blk + 1) * P)
-            return codes[i][:, cols].bitcast(FP8X4), xsc[i][:, cols]
-
-        def mx_pass(acc, g, mi, n):
-            lhsT, lhsT_scale = x_operand(g, mi)
             nc.tensor.matmul_mx(
                 out=acc[:],
-                lhsT=lhsT,
-                lhsT_scale=lhsT_scale,
+                lhsT=codes[i][:, cols].bitcast(FP8X4),
+                lhsT_scale=xsc[i][:, cols],
                 rhs=w[g][:, n * 2 * N_TILE : (n + 1) * 2 * N_TILE].bitcast(FP4X4),
-                rhs_scale=w_scale(g, n),
+                rhs_scale=plane_of[g][0][:, plane_of[g][1], n * N_TILE : (n + 1) * N_TILE],
                 start=(g == 0),
                 stop=(g == PASSES - 1),
             )
@@ -182,27 +142,19 @@ def tile_oddlayer_kernel(
                 nc.vector.tensor_copy(out=res[:], in_=acc[:])
             nc.sync.dma_start(out=out_rows[mi, :, n * N_TILE : (n + 1) * N_TILE], in_=res[:])
 
+        tiles = [(mi, n) for half in (0, 2) for mi in (0, 1) for n in (half, half + 1)]
         accs = [
             psum.tile([P, N_TILE], F32, name="accA%d" % j, tag="bank%d" % BANKS[j]) for j in range(8)
         ]
         for g in range(PASSES):
-            for j, (mi, n) in enumerate(ROUND_A):
+            for j, (mi, n) in enumerate(tiles):
                 mx_pass(accs[j], g, mi, n)
-        for j, (mi, n) in enumerate(ROUND_A):
+        for j, (mi, n) in enumerate(tiles):
             finish(accs[j], mi, n, j)
 
-        for s, mi in enumerate((2, 3)):
-            flip(1 + mi, (BANKS[2 * s], BANKS[2 * s + 1]), sorted_cols(sorted_words[s]))
-        quantise(3)
-        quantise(4)
-
-        accs = [
-            psum.tile([P, N_TILE], F32, name="accB%d" % j, tag="bank%d" % BANKS[b])
-            for j, (mi, n, b) in enumerate(ROUND_B)
-        ]
-        for j, (mi, n, b) in enumerate(ROUND_B):
-            mx_pass(accs[j], 0, mi, n)
-        for j, (mi, n, b) in enumerate(ROUND_B):
-            for g in range(1, PASSES):
-                mx_pass(accs[j], g, mi, n)
-            finish(accs[j], mi, n, j)
+        tiles = [(mi, n) for mi in (2, 3) for n in range(4)]
+        for j, (mi, n) in enumerate(tiles):
+            acc = psum.tile([P, N_TILE], F32, name="accB%d" % j, tag="bank%d" % BANKS[j])
+            for g in range(PASSES):
+                mx_pass(acc, g, mi, n)
+            finish(acc, mi, n, j)

from contextlib import ExitStack

import concourse.mybir as mybir
from concourse.masks import make_identity

F32 = mybir.dt.float32
BF16 = mybir.dt.bfloat16
I32 = mybir.dt.int32
U32 = mybir.dt.uint32
U8 = mybir.dt.uint8
FP8X4 = mybir.dt.float8_e4m3fn_x4
FP4X4 = mybir.dt.float4_e2m1fn_x4

P = 128
BATCH = 512
K_IN = 512
K_PREV = 2048
N_OUT = 2048
N_TILE = 512
M_TILES = BATCH // P
PASSES = (K_IN + K_PREV) // 512
FLOPS = 2 * BATCH * (K_IN + K_PREV) * N_OUT

BANKS = (2, 3, 4, 5, 6, 7, 0, 1)
SCALE_GROUPS = ((0, 1), (1, 2), (2, 3), (3, 5))


def tile_oddlayer_kernel(
    tc,
    x_in,
    x_prev,
    input_mask_words,
    input_mask_scales,
    prev_mask_words,
    prev_mask_scales,
    out,
):
    nc = tc.nc
    with ExitStack() as ctx:
        keep = ctx.enter_context(tc.tile_pool(name="keep", bufs=1))
        psum = ctx.enter_context(tc.psum_pool(name="psum", bufs=1))
        ctx.enter_context(tc.manual_schedule())

        ident = keep.tile([P, P], F32, name="ident")
        make_identity(nc, ident[:])

        plane_of = []
        for g0, g1 in SCALE_GROUPS:
            planes = keep.tile([P, g1 - g0, N_OUT], U8, name="planes%d" % g0, align_bytes=64)
            nc.vector.memset(planes[:].rearrange("p g n -> p (g n)").bitcast(I32), 0)
            plane_of.extend([(planes, g - g0) for g in range(g0, g1)])

        xp_rows = x_prev.rearrange("(p a) k -> a p k", a=M_TILES)
        out_rows = out.rearrange("(p a) n -> a p n", a=M_TILES)
        xin_raw = keep.tile([P, M_TILES, K_IN], BF16, name="xin_raw")
        xp_raw = [keep.tile([P, K_PREV], BF16, name="xp_raw%d" % mi) for mi in range(M_TILES)]
        w = [keep.tile([P, 2 * N_OUT], U8, name="w%d" % g, align_bytes=64) for g in range(PASSES)]

        def load_scales(g0, g1):
            src = input_mask_scales if g0 == 0 else prev_mask_scales[g0 - 1 : g1 - 1, :, :]
            planes = plane_of[g0][0]
            for r in range(4):
                nc.sync.dma_start(
                    out=planes[r:P:32, :, :].bitcast(I32),
                    in_=src[:, r:16:4, :].rearrange("g q n -> q g n").bitcast(I32),
                )

        def load_words(g, lo, hi):
            src = input_mask_words[0, :, :] if g == 0 else prev_mask_words[g - 1, :, :]
            nc.sync.dma_start(out=w[g][:, lo:hi].bitcast(I32), in_=src[:, lo:hi].bitcast(I32))

        nc.sync.dma_start(out=xin_raw[:], in_=x_in.rearrange("(p a) k -> p a k", a=M_TILES))
        for mi in range(M_TILES):
            nc.sync.dma_start(out=xp_raw[mi][:], in_=xp_rows[mi, :, :])
        load_scales(0, 1)
        load_words(0, 0, N_OUT)
        load_words(0, N_OUT, 2 * N_OUT)
        load_scales(1, 2)
        load_words(1, 0, N_OUT)
        load_words(1, N_OUT, 2 * N_OUT)
        load_scales(2, 3)
        load_words(2, 0, 2 * N_OUT)
        load_scales(3, 5)
        load_words(3, 0, 2 * N_OUT)
        load_words(4, 0, 2 * N_OUT)

        grouped = [keep.tile([P, 2048], BF16, name="grouped%d" % i, align_bytes=64) for i in range(5)]
        codes = [keep.tile([P, 512], U32, name="codes%d" % i, align_bytes=64) for i in range(5)]
        xsc = [keep.tile([P, 512], U8, name="xsc%d" % i, align_bytes=64) for i in range(5)]

        def quantise(i):
            nc.vector.quantize_mx(out=codes[i][:].bitcast(FP8X4), scales=xsc[i][:], in_=grouped[i][:])

        for i in range(5):
            for half in range(2):
                pt = psum.tile(
                    [P, 2, 2, P], F32, name="pt%d_%d" % (i, half), tag="bank%d" % ((2 * i + half) % 8)
                )
                for a in range(2):
                    blk = 2 * half + a
                    if i == 0:
                        words = xin_raw[:, blk, :].bitcast(F32)
                    else:
                        words = xp_raw[i - 1][:, 512 * blk : 512 * (blk + 1)].bitcast(F32)
                    for u in range(2):
                        nc.tensor.transpose(pt[:, a, u, :], words[:, u:256:2], ident[:])
                dst = (
                    grouped[i][:]
                    .bitcast(F32)[:, 512 * half : 512 * (half + 1)]
                    .rearrange("p (a m u) -> p a m u", a=2, u=2)
                )
                src = pt[:].rearrange("p a u m -> p a m u")
                if half == 0:
                    nc.scalar.copy(out=dst, in_=src)
                else:
                    nc.vector.tensor_copy(out=dst, in_=src)
            if i > 0:
                quantise(i - 1)
        quantise(4)

        def mx_pass(acc, g, mi, n):
            if g == 0:
                i, blk = 0, mi
            else:
                i, blk = 1 + mi, g - 1
            cols = slice(blk * P, (blk + 1) * P)
            nc.tensor.matmul_mx(
                out=acc[:],
                lhsT=codes[i][:, cols].bitcast(FP8X4),
                lhsT_scale=xsc[i][:, cols],
                rhs=w[g][:, n * 2 * N_TILE : (n + 1) * 2 * N_TILE].bitcast(FP4X4),
                rhs_scale=plane_of[g][0][:, plane_of[g][1], n * N_TILE : (n + 1) * N_TILE],
                start=(g == 0),
                stop=(g == PASSES - 1),
            )

        def finish(acc, mi, n, j):
            res = keep.tile([P, N_TILE], F32, name="res%d_%d" % (mi, n))
            if j % 2 == 0:
                nc.scalar.copy(out=res[:], in_=acc[:])
            else:
                nc.vector.tensor_copy(out=res[:], in_=acc[:])
            nc.sync.dma_start(out=out_rows[mi, :, n * N_TILE : (n + 1) * N_TILE], in_=res[:])

        tiles = [(mi, n) for half in (0, 2) for mi in (0, 1) for n in (half, half + 1)]
        accs = [
            psum.tile([P, N_TILE], F32, name="accA%d" % j, tag="bank%d" % BANKS[j]) for j in range(8)
        ]
        for g in range(PASSES):
            for j, (mi, n) in enumerate(tiles):
                mx_pass(accs[j], g, mi, n)
        for j, (mi, n) in enumerate(tiles):
            finish(accs[j], mi, n, j)

        tiles = [(mi, n) for mi in (2, 3) for n in range(4)]
        for j, (mi, n) in enumerate(tiles):
            acc = psum.tile([P, N_TILE], F32, name="accB%d" % j, tag="bank%d" % BANKS[j])
            for g in range(PASSES):
                mx_pass(acc, g, mi, n)
            finish(acc, mi, n, j)
